import numpy as np
import ml_dtypes


def mxq(x, axis, fmt="e4m3"):
    dtype, down = {"e4m3": (ml_dtypes.float8_e4m3fn, 7), "e5m2": (ml_dtypes.float8_e5m2, 14)}[fmt]
    v = np.moveaxis(np.asarray(x, np.float32).astype(ml_dtypes.bfloat16).astype(np.float64), axis, -1)
    blocks = v.reshape(v.shape[:-1] + (-1, 32))
    amax = np.abs(blocks).max(-1, keepdims=True)
    byte = np.maximum(np.where(amax > 0, np.frexp(amax)[1] - 1 + 127, 0) - down, 1)
    scale = np.exp2(byte - 127.0)
    codes = (blocks / scale).astype(np.float32).astype(dtype).astype(np.float64)
    return np.moveaxis((codes * scale).reshape(v.shape), -1, axis)


WIDE = False


def mx_kscale(k):
    if not WIDE:
        return np.ones(k)
    levels = np.array([30, -30])
    if k % 512:
        return np.exp2(np.random.permutation(np.resize(levels, k // 32))).repeat(32)
    a = np.empty((k // 512, 16))
    for p in range(k // 512):
        a[p, :8] = np.random.permutation(np.resize(levels, 8))
        for g in range(8):
            far = levels[np.abs(levels - a[p, g]) >= 10]
            a[p, g + 8] = far[np.random.randint(len(far))]
    return np.exp2(a.ravel()).repeat(32)


BF16 = ml_dtypes.bfloat16


def bf(x):
    return np.asarray(x, np.float32).astype(BF16)


def f64(x):
    return np.asarray(x).astype(np.float64)


B, T, C, H = 4, 128, 2048, 32
HD = C // H


def rotary_pos_emb(v):
    exponents = f64(np.arange(0, HD, 2)[: HD // 2] // HD)
    freqs = 1.0 / np.power(1000.0, exponents)
    theta = f64(np.arange(T))[:, None] * freqs[None, :]
    cos = np.cos(theta)[None, :, None, :]
    sin = np.sin(theta)[None, :, None, :]
    vr = v.reshape(B, T, H, HD // 2, 2)
    v0, v1 = vr[..., 0], vr[..., 1]
    out = np.stack([v0 * cos - v1 * sin, v0 * sin + v1 * cos], axis=-1)
    return out.reshape(B, T, H, HD)


def setup_inputs():
    s = mx_kscale(C)
    return {"x": bf(np.random.standard_normal((B, T, C)) * s),
            "wq": bf(np.random.standard_normal((C, C)) / np.sqrt(C) / s[None, :]),
            "wk": bf(np.random.standard_normal((C, C)) / np.sqrt(C) / s[None, :])}


def reference(x, wq, wk):
    xm = mxq(f64(x), 2, "e5m2")
    q = (xm @ mxq(f64(wq), 1, "e5m2").T).reshape(B, T, H, HD)
    k = (xm @ mxq(f64(wk), 1, "e5m2").T).reshape(B, T, H, HD)
    return rotary_pos_emb(q), rotary_pos_emb(k)

import math
from contextlib import ExitStack

import concourse.mybir as mybir
from concourse.masks import make_identity

B, T, C = 4, 128, 2048
FLOPS = 2 * 2 * B * T * C * C

F32 = mybir.dt.float32
BF16 = mybir.dt.bfloat16
U32 = mybir.dt.uint32
U8 = mybir.dt.uint8
FP8X4 = mybir.dt.float8_e5m2_x4
ALU = mybir.AluOpType
ACT = mybir.ActivationFunctionType

P = 128
PASSES = 4
PASS_WORDS = 256
N_TILE = 512
N_TILES = 2 * C // N_TILE
LOAD_AHEAD = 6
TURNS = 21
HALF_PI_HIGH = 201.0 / 128.0
HALF_PI_LOW = math.pi / 2 - HALF_PI_HIGH


def rotation_factors(nc, pool):
    position = pool.tile([P, 1], F32)
    nc.gpsimd.iota(position[:], [[0, 1]], base=0, channel_multiplier=1, allow_small_or_imprecise_dtypes=True)
    shift = pool.tile([P, 2], F32)
    nc.gpsimd.iota(shift[:], [[1, 2]], base=0, channel_multiplier=0, allow_small_or_imprecise_dtypes=True)
    edges = pool.tile([P, 2, TURNS], F32)
    nc.gpsimd.iota(
        edges[:], [[-1, 2], [4, TURNS]], base=2, channel_multiplier=0, allow_small_or_imprecise_dtypes=True
    )
    passed = pool.tile([P, 2, TURNS], F32)
    nc.vector.tensor_scalar(passed[:], edges[:], math.pi / 2, position[:], op0=ALU.mult, op1=ALU.is_le)
    turns = pool.tile([P, 2], F32)
    nc.vector.tensor_reduce(out=turns[:], in_=passed[:], op=ALU.add, axis=mybir.AxisListType.X)
    quarters = pool.tile([P, 2], F32)
    nc.vector.scalar_tensor_tensor(quarters[:], turns[:], -4.0, shift[:], op0=ALU.mult, op1=ALU.add)
    coarse = pool.tile([P, 2], F32)
    nc.vector.tensor_scalar(coarse[:], quarters[:], HALF_PI_HIGH, position[:], op0=ALU.mult, op1=ALU.add)
    angle = pool.tile([P, 2], F32)
    nc.vector.scalar_tensor_tensor(angle[:], quarters[:], HALF_PI_LOW, coarse[:], op0=ALU.mult, op1=ALU.add)
    sin_cos = pool.tile([P, 2], F32)
    nc.scalar.activation(sin_cos[:], angle[:], ACT.Sin)
    minus_sin = pool.tile([P, 1], F32)
    nc.scalar.activation(minus_sin[:], angle[:, 0:1], ACT.Sin, scale=-1.0)
    return sin_cos[:, 0:1], sin_cos[:, 1:2], minus_sin[:]


def tile_attention_pa_kernel(tc, x, wq, wk, out_0, out_1):
    nc = tc.nc
    tiles_per_weight = C // N_TILE
    weights = [wq, wk]
    outs = [o.rearrange("b t h d -> b t (h d)") for o in (out_0, out_1)]

    steps = [[("x", m), ("w", m)] for m in range(B)]
    steps += [[("w", n), ("w", n + 1)] for n in range(PASSES, N_TILES * PASSES, 2)]

    with ExitStack() as ctx:
        const = ctx.enter_context(tc.tile_pool(name="const", bufs=1))
        head = ctx.enter_context(tc.tile_pool(name="head", bufs=2 * B))
        stream = ctx.enter_context(tc.tile_pool(name="stream", bufs=LOAD_AHEAD + 1))
        stage = ctx.enter_context(tc.tile_pool(name="stage", bufs=4))
        x_keep = ctx.enter_context(tc.tile_pool(name="x_keep", bufs=B))
        w_keep = ctx.enter_context(tc.tile_pool(name="w_keep", bufs=8))
        results = ctx.enter_context(tc.tile_pool(name="results", bufs=6))
        flip_banks = ctx.enter_context(tc.psum_pool(name="flip_banks", bufs=4))
        sum_banks = ctx.enter_context(tc.psum_pool(name="sum_banks", bufs=1))
        ctx.enter_context(tc.manual_schedule())

        raw = {}
        split = {}
        grouped = {}
        quantised = {}
        sums = {}
        crossed = {}

        def weight_rows(n):
            j = n // PASSES
            first = (j % tiles_per_weight) * N_TILE
            rows = weights[j // tiles_per_weight][first : first + N_TILE, :]
            return rows.rearrange("(i p) k -> p i k", p=P)

        def load(step):
            units = steps[step]
            if units[0][0] == "x":
                m = units[0][1]
                x_raw = head.tile([P, PASSES, 2 * PASS_WORDS], BF16, tag="raw", name="x_raw")
                nc.sync.dma_start(out=x_raw[:].rearrange("p g k -> p (g k)"), in_=x[m])
                raw[units[0]] = x_raw[:].bitcast(F32)
                w_raw = head.tile([P, PASSES, 2 * PASS_WORDS], BF16, tag="raw", name="w_raw")
                nc.sync.dma_start(out=w_raw[:], in_=weight_rows(m)[:, :, 512 * m : 512 * (m + 1)])
                raw[units[1]] = w_raw[:].bitcast(F32)
            else:
                n = units[0][1]
                g = n % PASSES
                pair = stream.tile([P, 4, 4 * PASS_WORDS], BF16)
                nc.sync.dma_start(out=pair[:], in_=weight_rows(n)[:, :, 512 * g : 512 * (g + 2)])
                words = pair[:].bitcast(F32)
                raw[units[0]] = words[:, :, :PASS_WORDS]
                raw[units[1]] = words[:, :, PASS_WORDS:]

        def split_words(unit):
            halves = stage.tile([P, 4, 2, P], F32)
            nc.vector.tensor_copy(out=halves[:], in_=raw.pop(unit).rearrange("r i (p u) -> r i u p", u=2))
            split[unit] = halves

        def flip(unit):
            halves = split.pop(unit)
            k_on_partitions = stage.tile([P, 4 * P * 4], BF16, align_bytes=64)
            words = k_on_partitions[:].bitcast(F32).rearrange("p (i r u) -> p i r u", i=4, u=2)
            for h in range(2):
                bank = flip_banks.tile([P, 2, 2, P], F32)
                for i in range(2):
                    for u in range(2):
                        nc.tensor.transpose(bank[:, i, u, :], halves[:, 2 * h + i, u, :], identity[:])
                nc.scalar.copy(out=words[:, 2 * h : 2 * h + 2], in_=bank[:].rearrange("p i u r -> p i r u"))
            grouped[unit] = k_on_partitions

        def quantise(unit):
            pool = x_keep if unit[0] == "x" else w_keep
            codes = pool.tile([P, 4 * P], U32, align_bytes=64)
            scales = pool.tile([P, 4 * P], U8, align_bytes=64)
            nc.vector.quantize_mx(out=codes[:].bitcast(FP8X4), scales=scales[:], in_=grouped.pop(unit)[:])
            quantised[unit] = (codes, scales)

        def multiply(m, n):
            g = n % PASSES
            if g == 0:
                sums[m] = sum_banks.tile([P, N_TILE], F32, tag="sum%d" % m, name="sum%d" % m)
            x_codes, x_scales = quantised[("x", m)]
            w_codes, w_scales = quantised[("w", n)]
            nc.tensor.matmul_mx(
                out=sums[m][:],
                lhsT=x_codes[:, g * P : (g + 1) * P].bitcast(FP8X4),
                lhsT_scale=x_scales[:, g * P : (g + 1) * P],
                rhs=w_codes[:].bitcast(FP8X4),
                rhs_scale=w_scales[:],
                start=(g == 0),
                stop=(g == PASSES - 1),
            )

        def sine_terms(m):
            pairs = sums[m][:].rearrange("t (i e) -> t i e", e=2)
            terms = stage.tile([P, 2, N_TILE // 2], F32)
            nc.scalar.activation(terms[:, 0, :], pairs[:, :, 1], ACT.Copy, scale=minus_sin)
            nc.scalar.activation(terms[:, 1, :], pairs[:, :, 0], ACT.Copy, scale=sin)
            crossed[m] = terms

        def rotate_and_store(m, j):
            rotated = results.tile([P, N_TILE // 2, 2], F32)
            nc.vector.scalar_tensor_tensor(
                rotated[:],
                sums[m][:].rearrange("t (i e) -> t i e", e=2),
                cos,
                crossed.pop(m)[:].rearrange("t e i -> t i e"),
                op0=ALU.mult,
                op1=ALU.add,
            )
            first = (j % tiles_per_weight) * N_TILE
            nc.sync.dma_start(
                out=outs[j // tiles_per_weight][m][:, first : first + N_TILE],
                in_=rotated[:].rearrange("t i e -> t (i e)"),
            )

        for step in range(LOAD_AHEAD):
            load(step)
        identity = const.tile([P, P], F32)
        make_identity(nc, identity[:])
        sin, cos, minus_sin = rotation_factors(nc, const)
        for unit in steps[0]:
            split_words(unit)

        done = [0] * B
        ready = [0, 0]
        held = []
        for step in range(len(steps) + 1):
            last = step == len(steps)
            units = [] if last else steps[step]
            if step + LOAD_AHEAD < len(steps):
                load(step + LOAD_AHEAD)
            for m, j in held:
                rotate_and_store(m, j)
            if step + 1 < len(steps):
                for unit in steps[step + 1]:
                    split_words(unit)
            for unit in units:
                flip(unit)

            goal = [ready[-1] if (m < B // 2 or last) else ready[-2] for m in range(B)]
            active = [m for m in range(B) if ("x", m) in quantised and done[m] < goal[m]]
            closing = [m for m in active if goal[m] % PASSES == 0]
            for unit in units:
                quantise(unit)
            for m in closing + [m for m in active if m not in closing]:
                for n in range(done[m], goal[m]):
                    multiply(m, n)
                done[m] = goal[m]
            finished = [(m, goal[m] // PASSES - 1) for m in closing]
            for m, j in finished:
                sine_terms(m)
            keep_back = 0 if last else 1
            for m, j in finished[: len(finished) - keep_back]:
                rotate_and_store(m, j)
            held = finished[len(finished) - keep_back :]
            ready.append(ready[-1] + sum(1 for unit in units if unit[0] == "w"))
